import numpy as np
import ml_dtypes


BF16 = ml_dtypes.bfloat16


def bf(x):
    return np.asarray(x, np.float32).astype(BF16)


def f64(x):
    return np.asarray(x).astype(np.float64)


E2M1 = np.array([0.0, 0.5, 1.0, 1.5, 2.0, 3.0, 4.0, 6.0, -0.0, -0.5, -1.0, -1.5, -2.0, -3.0, -4.0, -6.0])


def pack_weight(w, fmt):
    k, n = w.shape
    w = f64(bf(w)).reshape(k // 32, 32, n)
    amax = np.abs(w).max(1)
    if fmt == "e4m3":
        byte = np.frexp(amax)[1] - 1 + 127 - 7
    else:
        mant, ex = np.frexp(amax / 6.0)
        byte = np.where(mant > 0.5, ex, ex - 1) + 127
    byte = np.clip(np.where(amax > 0, byte, 1), 1, 254)
    scaled = (w * np.exp2(127.0 - byte)[:, None, :]).reshape(k, n).astype(np.float32)
    by_word = np.ascontiguousarray(scaled.reshape(k // 512, 128, 4, n).transpose(0, 1, 3, 2))
    if fmt == "e4m3":
        words = by_word.astype(ml_dtypes.float8_e4m3fn).view(np.uint8)
    else:
        c = by_word.astype(ml_dtypes.float4_e2m1fn).view(np.uint8) & 0xF
        words = c[..., 0::2] | (c[..., 1::2] << 4)
    return np.ascontiguousarray(words), np.ascontiguousarray(byte.astype(np.uint8).reshape(k // 512, 16, n))


def unpack_weight(words, scales, fmt):
    g, p, n, _ = words.shape
    if fmt == "e4m3":
        vals = np.ascontiguousarray(words).view(ml_dtypes.float8_e4m3fn).astype(np.float64)
    else:
        nib = np.empty((g, p, n, 4), np.uint8)
        nib[..., 0::2] = words & 0xF
        nib[..., 1::2] = words >> 4
        vals = E2M1[nib]
    vals = vals * np.repeat(np.exp2(scales.astype(np.float64) - 127.0), 8, axis=1)[..., None]
    return vals.transpose(0, 1, 3, 2).reshape(g * 512, n)

def pack4(w):
    words, scales = pack_weight(w, "e2m1")
    return words.reshape(words.shape[0], 128, -1), scales


def unpack4(words, scales):
    return unpack_weight(words.reshape(words.shape[0], 128, -1, 2), scales, "e2m1")


def kspread(k):
    return np.exp2(np.repeat(np.random.randint(-6, 7, k // 32), 32).astype(np.float64))


N, S, D, H = 4, 128, 5120, 8
L = N * S
DH = D // H


def rope(t, cos, sin):
    tr = t[..., 0::2]
    ti = t[..., 1::2]
    c = cos[:, None, :]
    s = sin[:, None, :]
    out_r = tr * c - ti * s
    out_i = tr * s + ti * c
    return np.stack([out_r, out_i], axis=-1).reshape(t.shape)


def setup_inputs():
    s = kspread(D)
    ang = np.random.uniform(0.0, 2.0 * np.pi, (L, DH // 2))
    x = np.random.standard_normal((L, D)) * s
    x_words, x_scales = pack4(x.reshape(L, D).T)
    words, scales = pack4(np.random.standard_normal((D, 2 * D)) * 1.5 / np.sqrt(D) / s[:, None])
    b_qk = bf(np.random.standard_normal(2 * D) * 0.1)
    return {"x_words": x_words, "x_scales": x_scales,
            "w_qk_words": words, "w_qk_scales": scales,
            "b_qk": b_qk,
            "freqs_cos": bf(np.cos(ang)), "freqs_sin": bf(np.sin(ang))}


def reference(x_words, x_scales, w_qk_words, w_qk_scales, b_qk, freqs_cos, freqs_sin):
    qk = (unpack4(x_words, x_scales).T @ unpack4(w_qk_words, w_qk_scales)) + f64(b_qk)
    q, k = [t.reshape(L, H, DH) for t in np.split(qk, 2, axis=-1)]
    c, s = f64(freqs_cos), f64(freqs_sin)
    return rope(q, c, s), rope(k, c, s)

from contextlib import ExitStack

import concourse.mybir as mybir

TOKENS, K, CHANNELS = 512, 5120, 10240
HALF = CHANNELS // 2
HEAD = 640
PAIRS = HEAD // 2

FLOPS = 2 * TOKENS * K * CHANNELS

F32 = mybir.dt.float32
BF16 = mybir.dt.bfloat16
I32 = mybir.dt.int32
U8 = mybir.dt.uint8
FP4X4 = mybir.dt.float4_e2m1fn_x4
ADD = mybir.AluOpType.add
MULT = mybir.AluOpType.mult

P = 128
PASSES = K // 512
TOKEN_TILES = TOKENS // P
BANK = 512
BLOCK = 1024
BLOCKS = CHANNELS // BLOCK
TABLE = 1536
W_BUFS = 3


def tile_moonvitvisiontower_pa_kernel(
    tc, x_words, x_scales, w_qk_words, w_qk_scales, b_qk, freqs_cos, freqs_sin, out_0, out_1
):
    nc = tc.nc
    outs = [o.rearrange("l h d -> l (h d)") for o in (out_0, out_1)]

    with ExitStack() as ctx:
        keep = ctx.enter_context(tc.tile_pool(name="keep", bufs=1))
        w_pool = ctx.enter_context(tc.tile_pool(name="w", bufs=W_BUFS))
        work = ctx.enter_context(tc.tile_pool(name="work", bufs=2))
        psum = ctx.enter_context(tc.psum_pool(name="psum", bufs=1))
        ctx.enter_context(tc.manual_schedule())

        x_codes = keep.tile([P, PASSES, 2 * TOKENS], U8, name="x_codes", align_bytes=256)
        x_planes = keep.tile([P, PASSES, TOKENS], U8, name="x_planes", align_bytes=256)
        w_planes = [
            keep.tile([P, PASSES, BLOCK], U8, name="w_planes%d" % i, align_bytes=256) for i in range(W_BUFS)
        ]
        bias = keep.tile([P, CHANNELS], BF16, name="bias")
        cos_raw = keep.tile([P, TOKEN_TILES, PAIRS], BF16, name="cos_raw")
        sin_raw = keep.tile([P, TOKEN_TILES, PAIRS], BF16, name="sin_raw")
        table = keep.tile([P, TOKEN_TILES, 2, TABLE], BF16, name="table")
        sign = keep.tile([P, 2], BF16, name="sign")

        def zero(planes, g0, g1):
            nc.vector.memset(planes[:, g0:g1, :].bitcast(I32), 0)

        def load_x_codes(g0, g1):
            nc.sync.dma_start(
                out=x_codes[:, g0:g1, :].bitcast(I32),
                in_=x_words[g0:g1].rearrange("g p b -> p g b").bitcast(I32),
            )

        def load_x_scales(g0, g1):
            for q in range(4):
                nc.sync.dma_start(
                    out=x_planes[32 * q : 32 * q + 4, g0:g1, :].bitcast(I32),
                    in_=x_scales[g0:g1, 4 * q : 4 * q + 4, :].rearrange("g r n -> r g n").bitcast(I32),
                )

        def load_w_codes(codes, block, g0, g1):
            nc.sync.dma_start(
                out=codes[:, g0:g1, :].bitcast(I32),
                in_=w_qk_words[g0:g1, :, 2 * BLOCK * block : 2 * BLOCK * (block + 1)]
                .rearrange("g p b -> p g b")
                .bitcast(I32),
            )

        def load_w_scales(block, g0, g1):
            planes = w_planes[block % W_BUFS]
            for q in range(4):
                nc.sync.dma_start(
                    out=planes[32 * q : 32 * q + 4, g0:g1, :].bitcast(I32),
                    in_=w_qk_scales[g0:g1, 4 * q : 4 * q + 4, BLOCK * block : BLOCK * (block + 1)]
                    .rearrange("g r n -> r g n")
                    .bitcast(I32),
                )

        def matmul(acc, codes, block, m, col, width, g):
            nc.tensor.matmul_mx(
                out=acc[:, 0:width],
                lhsT=x_codes[:, g, 2 * P * m : 2 * P * (m + 1)].bitcast(FP4X4),
                lhsT_scale=x_planes[:, g, P * m : P * (m + 1)],
                rhs=codes[:, g, 2 * col : 2 * (col + width)].bitcast(FP4X4),
                rhs_scale=w_planes[block % W_BUFS][:, g, col : col + width],
                start=(g == 0),
                stop=(g == PASSES - 1),
            )

        def bank(i):
            return psum.tile([P, BANK], F32, name="bank%d" % i)

        def new_codes():
            return w_pool.tile([P, PASSES, 2 * BLOCK], U8, name="w_codes", align_bytes=256)

        codes = {0: new_codes(), 1: new_codes()}
        zero(x_planes, 0, 2)
        zero(w_planes[0], 0, 2)
        load_x_codes(0, 1)
        load_w_codes(codes[0], 0, 0, 1)
        load_x_scales(0, 2)
        load_w_scales(0, 0, 2)
        load_w_codes(codes[0], 0, 1, 2)
        load_x_codes(1, 2)
        zero(x_planes, 2, 10)
        zero(w_planes[0], 2, 10)
        load_w_codes(codes[0], 0, 2, 5)
        load_x_codes(2, 5)
        load_x_scales(2, 5)
        load_w_scales(0, 2, 5)
        load_w_codes(codes[0], 0, 5, 10)
        load_x_codes(5, 10)
        load_x_scales(5, 10)
        load_w_scales(0, 5, 10)
        for tile_, src in ((cos_raw, freqs_cos), (sin_raw, freqs_sin)):
            nc.sync.dma_start(out=tile_[:], in_=src.rearrange("(m p) j -> p m j", p=P))
        nc.sync.dma_start(out=bias[:, 0:2048], in_=b_qk[0:2048].partition_broadcast(P))
        zero(w_planes[1], 0, 10)
        load_w_codes(codes[1], 1, 0, 5)
        load_w_scales(1, 0, 10)
        load_w_codes(codes[1], 1, 5, 10)
        nc.sync.dma_start(out=bias[:, 2048:], in_=b_qk[2048:].partition_broadcast(P))
        zero(w_planes[2], 0, 10)

        nc.vector.memset(sign[:, 0:1], 1.0)
        nc.vector.memset(sign[:, 1:2], -1.0)
        for m in range(TOKEN_TILES):
            for c0, reps, pairs in ((0, 2, PAIRS), (2 * HEAD, 1, TABLE // 2 - 2 * PAIRS)):
                shape = [P, reps, pairs, 2]
                cols = slice(c0, c0 + 2 * reps * pairs)
                nc.scalar.copy(
                    out=table[:, m, 0, cols].rearrange("p (r j t) -> p r j t", r=reps, t=2),
                    in_=cos_raw[:, m, 0:pairs].unsqueeze(1).unsqueeze(3).to_broadcast(shape),
                )
                nc.vector.tensor_tensor(
                    out=table[:, m, 1, cols].rearrange("p (r j t) -> p r j t", r=reps, t=2),
                    in0=sin_raw[:, m, 0:pairs].unsqueeze(1).unsqueeze(3).to_broadcast(shape),
                    in1=sign[:].unsqueeze(1).unsqueeze(1).to_broadcast(shape),
                    op=MULT,
                )

        def add_bias(job):
            width = sum(w for (acc, w) in job["parts"])
            job["width"] = width
            y = work.tile([P, BLOCK], F32, name="y")
            job["y"] = y
            off = 0
            for acc, w in job["parts"]:
                c = job["c0"] + off
                nc.vector.tensor_tensor(out=y[:, off : off + w], in0=acc[:, 0:w], in1=bias[:, c : c + w], op=ADD)
                off += w

        def products(job):
            width = job["width"]
            prod = work.tile([P, 2, BLOCK], F32, name="prod")
            job["prod"] = prod
            t0 = (job["c0"] % HALF) % HEAD
            nc.vector.tensor_tensor(
                out=prod[:, :, 0:width],
                in0=job["y"][:, 0:width].unsqueeze(1).to_broadcast([P, 2, width]),
                in1=table[:, job["m"], :, t0 : t0 + width],
                op=MULT,
            )

        def finish(job):
            width, m, c0, prod = job["width"], job["m"], job["c0"], job["prod"]
            res = work.tile([P, BLOCK], F32, name="res", bufs=4)
            nc.vector.tensor_tensor(
                out=res[:, 0:width].rearrange("p (j t) -> p j t", t=2),
                in0=prod[:, 0, 0:width].rearrange("p (j t) -> p j t", t=2),
                in1=prod[:, 1, 0:width].rearrange("p (j t) -> p j t", t=2)[:, :, ::-1],
                op=ADD,
            )
            dst = outs[c0 // HALF][P * m : P * (m + 1), c0 % HALF : c0 % HALF + width]
            job["queue"].dma_start(out=dst, in_=res[:, 0:width])

        pending = []

        def epilogue(job):
            add_bias(job)
            if pending:
                finish(pending.pop())
            products(job)
            pending.append(job)

        for block in range(BLOCKS):
            c0 = BLOCK * block
            if block + 2 < BLOCKS:
                codes[block + 2] = new_codes()
                load_w_codes(codes[block + 2], block + 2, 0, 5)
                load_w_scales(block + 2, 0, 10)
                load_w_codes(codes[block + 2], block + 2, 5, 10)
            cb = codes[block]
            if block == 0:
                banks = [bank(i) for i in range(8)]
                for g in range(PASSES):
                    for m in range(TOKEN_TILES):
                        for n in range(2):
                            matmul(banks[2 * m + n], cb, block, m, BANK * n, BANK, g)
                for m in range(TOKEN_TILES):
                    epilogue(
                        {"m": m, "c0": c0, "parts": [(banks[2 * m], BANK), (banks[2 * m + 1], BANK)], "queue": nc.gpsimd}
                    )
            elif block < BLOCKS - 1:
                for m in range(TOKEN_TILES):
                    parts = []
                    for n in range(2):
                        acc = bank(2 * m + n)
                        for g in range(PASSES):
                            matmul(acc, cb, block, m, BANK * n, BANK, g)
                        parts.append((acc, BANK))
                    epilogue({"m": m, "c0": c0, "parts": parts, "queue": nc.gpsimd})
            else:
                pieces = [(m, BANK) for m in range(TOKEN_TILES - 1) for n in range(2)]
                pieces += [(TOKEN_TILES - 1, w) for w in (256, 256, 256, 128, 128)]
                col = 0
                for i, (m, width) in enumerate(pieces):
                    acc = bank(i % 8)
                    for g in range(PASSES):
                        matmul(acc, cb, block, m, col, width, g)
                    epilogue({"m": m, "c0": c0 + col, "parts": [(acc, width)], "queue": nc.sync})
                    col = (col + width) % BLOCK
        finish(pending.pop())
